import numpy as np
import ml_dtypes

BF16 = ml_dtypes.bfloat16


def bf(x):
    return np.asarray(x, np.float32).astype(BF16)


def f32(x):
    return np.asarray(x, np.float32)


def f64(x):
    return np.asarray(x).astype(np.float64)


def striped(idx):
    return np.tile(idx.reshape(-1, 16).T, (8, 1))


D, S, N = 128, 512, 128
SIGMA = 2.0


def setup_inputs():
    a = np.sqrt(SIGMA / np.sqrt(D))
    return {"keys": bf(a * np.random.standard_normal((D, S))), "queries": bf(a * np.random.standard_normal((D, S))), "offs": striped(np.random.permutation(S)[:N])}


def reference(keys, queries, offs):
    idx = offs[:16].T.reshape(-1)
    z = f64(queries).T @ f64(keys)[:, idx]
    e = np.exp(z - z.max(axis=1, keepdims=True))
    return e / e.sum(axis=1, keepdims=True)

@@ -1,0 +1,47 @@
+import concourse.mybir as mybir
+
+P = 128
+FLOPS = 2 * 128 * 512 * 128
+
+BF16, F32, U16 = mybir.dt.bfloat16, mybir.dt.float32, mybir.dt.uint16
+EXP = mybir.ActivationFunctionType.Exp
+ROW = mybir.AxisListType.X
+
+
+def tile_nystromattention_kernel(tc, keys, queries, offs, out):
+    nc = tc.nc
+    n_keys = keys.shape[1]
+    n_queries = queries.shape[1]
+    n_landmarks = out.shape[1]
+    n_blocks = n_queries // P
+
+    with (
+        tc.tile_pool(name="held", bufs=1) as held,
+        tc.tile_pool(name="work", bufs=n_blocks) as work,
+        tc.psum_pool(name="psum", bufs=n_blocks) as psum,
+    ):
+        offsets = held.tile([P, n_landmarks // 16], U16, name="offsets")
+        nc.sync.dma_start(offsets[:], offs)
+        keys_sb = held.tile([P, n_keys], BF16, name="keys_sb")
+        nc.sync.dma_start(keys_sb[:], keys)
+        queries_sb = held.tile([P, n_queries], BF16, name="queries_sb")
+        nc.scalar.dma_start(queries_sb[:], queries)
+
+        for b in range(n_blocks):
+            scores = psum.tile([P, n_landmarks], F32, name="scores")
+            nc.tensor.matmul(
+                scores[:],
+                queries_sb[:, b * P : (b + 1) * P],
+                keys_sb[:].indirect(offsets[:]),
+                start=True,
+                stop=True,
+            )
+            neg_max = work.tile([P, 1], F32, name="neg_max")
+            nc.vector.reduce_max(neg_max[:], scores[:], ROW, negate=True)
+            weights = work.tile([P, n_landmarks], F32, name="weights")
+            row_sum = work.tile([P, 1], F32, name="row_sum")
+            nc.scalar.activation(weights[:], scores[:], EXP, bias=neg_max[:], accum_out=row_sum[:])
+            inv_sum = work.tile([P, 1], F32, name="inv_sum")
+            nc.vector.reciprocal(inv_sum[:], row_sum[:])
+            nc.vector.tensor_scalar_mul(weights[:], weights[:], inv_sum[:])
+            nc.sync.dma_start(out[b * P : (b + 1) * P, :], weights[:])

@@ -3,6 +3,8 @@ import concourse.mybir as mybir
 P = 128
 FLOPS = 2 * 128 * 512 * 128
 
+N_WARM = 14
+
 BF16, F32, U16 = mybir.dt.bfloat16, mybir.dt.float32, mybir.dt.uint16
 EXP = mybir.ActivationFunctionType.Exp
 ROW = mybir.AxisListType.X
@@ -19,7 +21,14 @@ def tile_nystromattention_kernel(tc, keys, queries, offs, out):
         tc.tile_pool(name="held", bufs=1) as held,
         tc.tile_pool(name="work", bufs=n_blocks) as work,
         tc.psum_pool(name="psum", bufs=n_blocks) as psum,
+        tc.psum_pool(name="warm_psum", bufs=1) as warm_psum,
     ):
+        warm_in = held.tile([P, P], BF16, name="warm_in")
+        nc.vector.memset(warm_in[:], 0.0)
+        warm_out = warm_psum.tile([P, P], F32, name="warm_out")
+        for i in range(N_WARM):
+            nc.tensor.matmul(warm_out[:], warm_in[:], warm_in[:], start=True, stop=True)
+
         offsets = held.tile([P, n_landmarks // 16], U16, name="offsets")
         nc.sync.dma_start(offsets[:], offs)
         keys_sb = held.tile([P, n_keys], BF16, name="keys_sb")

@@ -3,8 +3,6 @@ import concourse.mybir as mybir
 P = 128
 FLOPS = 2 * 128 * 512 * 128
 
-N_WARM = 14
-
 BF16, F32, U16 = mybir.dt.bfloat16, mybir.dt.float32, mybir.dt.uint16
 EXP = mybir.ActivationFunctionType.Exp
 ROW = mybir.AxisListType.X
@@ -21,20 +19,14 @@ def tile_nystromattention_kernel(tc, keys, queries, offs, out):
         tc.tile_pool(name="held", bufs=1) as held,
         tc.tile_pool(name="work", bufs=n_blocks) as work,
         tc.psum_pool(name="psum", bufs=n_blocks) as psum,
-        tc.psum_pool(name="warm_psum", bufs=1) as warm_psum,
     ):
-        warm_in = held.tile([P, P], BF16, name="warm_in")
-        nc.vector.memset(warm_in[:], 0.0)
-        warm_out = warm_psum.tile([P, P], F32, name="warm_out")
-        for i in range(N_WARM):
-            nc.tensor.matmul(warm_out[:], warm_in[:], warm_in[:], start=True, stop=True)
-
         offsets = held.tile([P, n_landmarks // 16], U16, name="offsets")
         nc.sync.dma_start(offsets[:], offs)
         keys_sb = held.tile([P, n_keys], BF16, name="keys_sb")
         nc.sync.dma_start(keys_sb[:], keys)
         queries_sb = held.tile([P, n_queries], BF16, name="queries_sb")
-        nc.scalar.dma_start(queries_sb[:], queries)
+        nc.scalar.dma_start(queries_sb[:, :P], queries[:, :P])
+        nc.sync.dma_start(queries_sb[:, P:], queries[:, P:])
 
         for b in range(n_blocks):
             scores = psum.tile([P, n_landmarks], F32, name="scores")

@@ -23,10 +23,9 @@ def tile_nystromattention_kernel(tc, keys, queries, offs, out):
         offsets = held.tile([P, n_landmarks // 16], U16, name="offsets")
         nc.sync.dma_start(offsets[:], offs)
         keys_sb = held.tile([P, n_keys], BF16, name="keys_sb")
-        nc.sync.dma_start(keys_sb[:], keys)
+        nc.scalar.dma_start(keys_sb[:], keys)
         queries_sb = held.tile([P, n_queries], BF16, name="queries_sb")
-        nc.scalar.dma_start(queries_sb[:, :P], queries[:, :P])
-        nc.sync.dma_start(queries_sb[:, P:], queries[:, P:])
+        nc.scalar.dma_start(queries_sb[:], queries)
 
         for b in range(n_blocks):
             scores = psum.tile([P, n_landmarks], F32, name="scores")

@@ -23,9 +23,13 @@ def tile_nystromattention_kernel(tc, keys, queries, offs, out):
         offsets = held.tile([P, n_landmarks // 16], U16, name="offsets")
         nc.sync.dma_start(offsets[:], offs)
         keys_sb = held.tile([P, n_keys], BF16, name="keys_sb")
-        nc.scalar.dma_start(keys_sb[:], keys)
+        nc.sync.dma_start(keys_sb[:], keys)
         queries_sb = held.tile([P, n_queries], BF16, name="queries_sb")
         nc.scalar.dma_start(queries_sb[:], queries)
+
+        row_sums = held.tile([P, n_blocks], F32, name="row_sums")
+        inv_sums = held.tile([P, n_blocks], F32, name="inv_sums")
+        weights = []
 
         for b in range(n_blocks):
             scores = psum.tile([P, n_landmarks], F32, name="scores")
@@ -38,10 +42,12 @@ def tile_nystromattention_kernel(tc, keys, queries, offs, out):
             )
             neg_max = work.tile([P, 1], F32, name="neg_max")
             nc.vector.reduce_max(neg_max[:], scores[:], ROW, negate=True)
-            weights = work.tile([P, n_landmarks], F32, name="weights")
-            row_sum = work.tile([P, 1], F32, name="row_sum")
-            nc.scalar.activation(weights[:], scores[:], EXP, bias=neg_max[:], accum_out=row_sum[:])
-            inv_sum = work.tile([P, 1], F32, name="inv_sum")
-            nc.vector.reciprocal(inv_sum[:], row_sum[:])
-            nc.vector.tensor_scalar_mul(weights[:], weights[:], inv_sum[:])
-            nc.sync.dma_start(out[b * P : (b + 1) * P, :], weights[:])
+            weights.append(work.tile([P, n_landmarks], F32, name="weights"))
+            nc.scalar.activation(
+                weights[b][:], scores[:], EXP, bias=neg_max[:], accum_out=row_sums[:, b : b + 1]
+            )
+
+        nc.vector.reciprocal(inv_sums[:], row_sums[:])
+        for b in range(n_blocks):
+            nc.vector.tensor_scalar_mul(weights[b][:], weights[b][:], inv_sums[:, b : b + 1])
+            nc.sync.dma_start(out[b * P : (b + 1) * P, :], weights[b][:])

@@ -25,11 +25,7 @@ def tile_nystromattention_kernel(tc, keys, queries, offs, out):
         keys_sb = held.tile([P, n_keys], BF16, name="keys_sb")
         nc.sync.dma_start(keys_sb[:], keys)
         queries_sb = held.tile([P, n_queries], BF16, name="queries_sb")
-        nc.scalar.dma_start(queries_sb[:], queries)
-
-        row_sums = held.tile([P, n_blocks], F32, name="row_sums")
-        inv_sums = held.tile([P, n_blocks], F32, name="inv_sums")
-        weights = []
+        nc.sync.dma_start(queries_sb[:], queries)
 
         for b in range(n_blocks):
             scores = psum.tile([P, n_landmarks], F32, name="scores")
@@ -42,12 +38,10 @@ def tile_nystromattention_kernel(tc, keys, queries, offs, out):
             )
             neg_max = work.tile([P, 1], F32, name="neg_max")
             nc.vector.reduce_max(neg_max[:], scores[:], ROW, negate=True)
-            weights.append(work.tile([P, n_landmarks], F32, name="weights"))
-            nc.scalar.activation(
-                weights[b][:], scores[:], EXP, bias=neg_max[:], accum_out=row_sums[:, b : b + 1]
-            )
-
-        nc.vector.reciprocal(inv_sums[:], row_sums[:])
-        for b in range(n_blocks):
-            nc.vector.tensor_scalar_mul(weights[b][:], weights[b][:], inv_sums[:, b : b + 1])
-            nc.sync.dma_start(out[b * P : (b + 1) * P, :], weights[b][:])
+            weights = work.tile([P, n_landmarks], F32, name="weights")
+            row_sum = work.tile([P, 1], F32, name="row_sum")
+            nc.scalar.activation(weights[:], scores[:], EXP, bias=neg_max[:], accum_out=row_sum[:])
+            inv_sum = work.tile([P, 1], F32, name="inv_sum")
+            nc.vector.reciprocal(inv_sum[:], row_sum[:])
+            nc.vector.tensor_scalar_mul(weights[:], weights[:], inv_sum[:])
+            nc.sync.dma_start(out[b * P : (b + 1) * P, :], weights[:])

@@ -24,14 +24,14 @@ def tile_nystromattention_kernel(tc, keys, queries, offs, out):
         nc.sync.dma_start(offsets[:], offs)
         keys_sb = held.tile([P, n_keys], BF16, name="keys_sb")
         nc.sync.dma_start(keys_sb[:], keys)
-        queries_sb = held.tile([P, n_queries], BF16, name="queries_sb")
-        nc.sync.dma_start(queries_sb[:], queries)
 
         for b in range(n_blocks):
+            queries_sb = work.tile([P, P], BF16, name="queries_sb")
+            nc.sync.dma_start(queries_sb[:], queries[:, b * P : (b + 1) * P])
             scores = psum.tile([P, n_landmarks], F32, name="scores")
             nc.tensor.matmul(
                 scores[:],
-                queries_sb[:, b * P : (b + 1) * P],
+                queries_sb[:],
                 keys_sb[:].indirect(offsets[:]),
                 start=True,
                 stop=True,

@@ -5,7 +5,6 @@ FLOPS = 2 * 128 * 512 * 128
 
 BF16, F32, U16 = mybir.dt.bfloat16, mybir.dt.float32, mybir.dt.uint16
 EXP = mybir.ActivationFunctionType.Exp
-ROW = mybir.AxisListType.X
 
 
 def tile_nystromattention_kernel(tc, keys, queries, offs, out):
@@ -36,11 +35,9 @@ def tile_nystromattention_kernel(tc, keys, queries, offs, out):
                 start=True,
                 stop=True,
             )
-            neg_max = work.tile([P, 1], F32, name="neg_max")
-            nc.vector.reduce_max(neg_max[:], scores[:], ROW, negate=True)
             weights = work.tile([P, n_landmarks], F32, name="weights")
             row_sum = work.tile([P, 1], F32, name="row_sum")
-            nc.scalar.activation(weights[:], scores[:], EXP, bias=neg_max[:], accum_out=row_sum[:])
+            nc.scalar.activation(weights[:], scores[:], EXP, accum_out=row_sum[:])
             inv_sum = work.tile([P, 1], F32, name="inv_sum")
             nc.vector.reciprocal(inv_sum[:], row_sum[:])
             nc.vector.tensor_scalar_mul(weights[:], weights[:], inv_sum[:])

@@ -19,18 +19,19 @@ def tile_nystromattention_kernel(tc, keys, queries, offs, out):
         tc.tile_pool(name="work", bufs=n_blocks) as work,
         tc.psum_pool(name="psum", bufs=n_blocks) as psum,
     ):
-        offsets = held.tile([P, n_landmarks // 16], U16, name="offsets")
-        nc.sync.dma_start(offsets[:], offs)
         keys_sb = held.tile([P, n_keys], BF16, name="keys_sb")
         nc.sync.dma_start(keys_sb[:], keys)
 
+        queries_sb = held.tile([P, n_queries], BF16, name="queries_sb")
+        nc.sync.dma_start(queries_sb[:], queries)
+        offsets = held.tile([P, n_landmarks // 16], U16, name="offsets")
+        nc.sync.dma_start(offsets[:], offs)
+
         for b in range(n_blocks):
-            queries_sb = work.tile([P, P], BF16, name="queries_sb")
-            nc.sync.dma_start(queries_sb[:], queries[:, b * P : (b + 1) * P])
             scores = psum.tile([P, n_landmarks], F32, name="scores")
             nc.tensor.matmul(
                 scores[:],
-                queries_sb[:],
+                queries_sb[:, b * P : (b + 1) * P],
                 keys_sb[:].indirect(offsets[:]),
                 start=True,
                 stop=True,

@@ -21,17 +21,19 @@ def tile_nystromattention_kernel(tc, keys, queries, offs, out):
     ):
         keys_sb = held.tile([P, n_keys], BF16, name="keys_sb")
         nc.sync.dma_start(keys_sb[:], keys)
-
-        queries_sb = held.tile([P, n_queries], BF16, name="queries_sb")
-        nc.sync.dma_start(queries_sb[:], queries)
+        first_queries = held.tile([P, P], BF16, name="first_queries")
+        nc.sync.dma_start(first_queries[:], queries[:, 0:P])
         offsets = held.tile([P, n_landmarks // 16], U16, name="offsets")
         nc.sync.dma_start(offsets[:], offs)
+        other_queries = held.tile([P, n_queries - P], BF16, name="other_queries")
+        nc.sync.dma_start(other_queries[:], queries[:, P:n_queries])
 
         for b in range(n_blocks):
+            block_queries = first_queries[:] if b == 0 else other_queries[:, (b - 1) * P : b * P]
             scores = psum.tile([P, n_landmarks], F32, name="scores")
             nc.tensor.matmul(
                 scores[:],
-                queries_sb[:, b * P : (b + 1) * P],
+                block_queries,
                 keys_sb[:].indirect(offsets[:]),
                 start=True,
                 stop=True,

@@ -1,5 +1,6 @@
 import concourse.mybir as mybir
 
+ROW_ALIGN = 512
 P = 128
 FLOPS = 2 * 128 * 512 * 128
 
@@ -19,13 +20,13 @@ def tile_nystromattention_kernel(tc, keys, queries, offs, out):
         tc.tile_pool(name="work", bufs=n_blocks) as work,
         tc.psum_pool(name="psum", bufs=n_blocks) as psum,
     ):
-        keys_sb = held.tile([P, n_keys], BF16, name="keys_sb")
+        keys_sb = held.tile([P, n_keys], BF16, name="keys_sb", align_bytes=ROW_ALIGN)
         nc.sync.dma_start(keys_sb[:], keys)
-        first_queries = held.tile([P, P], BF16, name="first_queries")
+        first_queries = held.tile([P, P], BF16, name="first_queries", align_bytes=ROW_ALIGN)
         nc.sync.dma_start(first_queries[:], queries[:, 0:P])
-        offsets = held.tile([P, n_landmarks // 16], U16, name="offsets")
+        offsets = held.tile([P, n_landmarks // 16], U16, name="offsets", align_bytes=ROW_ALIGN)
         nc.sync.dma_start(offsets[:], offs)
-        other_queries = held.tile([P, n_queries - P], BF16, name="other_queries")
+        other_queries = held.tile([P, n_queries - P], BF16, name="other_queries", align_bytes=ROW_ALIGN)
         nc.sync.dma_start(other_queries[:], queries[:, P:n_queries])
 
         for b in range(n_blocks):
@@ -38,7 +39,7 @@ def tile_nystromattention_kernel(tc, keys, queries, offs, out):
                 start=True,
                 stop=True,
             )
-            weights = work.tile([P, n_landmarks], F32, name="weights")
+            weights = work.tile([P, n_landmarks], F32, name="weights", align_bytes=ROW_ALIGN)
             row_sum = work.tile([P, 1], F32, name="row_sum")
             nc.scalar.activation(weights[:], scores[:], EXP, accum_out=row_sum[:])
             inv_sum = work.tile([P, 1], F32, name="inv_sum")

@@ -40,9 +40,9 @@ def tile_nystromattention_kernel(tc, keys, queries, offs, out):
                 stop=True,
             )
             weights = work.tile([P, n_landmarks], F32, name="weights", align_bytes=ROW_ALIGN)
-            row_sum = work.tile([P, 1], F32, name="row_sum")
+            row_sum = work.tile([P, 1], F32, name="row_sum", align_bytes=ROW_ALIGN)
             nc.scalar.activation(weights[:], scores[:], EXP, accum_out=row_sum[:])
-            inv_sum = work.tile([P, 1], F32, name="inv_sum")
+            inv_sum = work.tile([P, 1], F32, name="inv_sum", align_bytes=ROW_ALIGN)
             nc.vector.reciprocal(inv_sum[:], row_sum[:])
             nc.vector.tensor_scalar_mul(weights[:], weights[:], inv_sum[:])
             nc.sync.dma_start(out[b * P : (b + 1) * P, :], weights[:])

import concourse.mybir as mybir

ROW_ALIGN = 512
P = 128
FLOPS = 2 * 128 * 512 * 128

BF16, F32, U16 = mybir.dt.bfloat16, mybir.dt.float32, mybir.dt.uint16
EXP = mybir.ActivationFunctionType.Exp


def tile_nystromattention_kernel(tc, keys, queries, offs, out):
    nc = tc.nc
    n_keys = keys.shape[1]
    n_queries = queries.shape[1]
    n_landmarks = out.shape[1]
    n_blocks = n_queries // P

    with (
        tc.tile_pool(name="held", bufs=1) as held,
        tc.tile_pool(name="work", bufs=n_blocks) as work,
        tc.psum_pool(name="psum", bufs=n_blocks) as psum,
    ):
        keys_sb = held.tile([P, n_keys], BF16, name="keys_sb", align_bytes=ROW_ALIGN)
        nc.sync.dma_start(keys_sb[:], keys)
        first_queries = held.tile([P, P], BF16, name="first_queries", align_bytes=ROW_ALIGN)
        nc.sync.dma_start(first_queries[:], queries[:, 0:P])
        offsets = held.tile([P, n_landmarks // 16], U16, name="offsets", align_bytes=ROW_ALIGN)
        nc.sync.dma_start(offsets[:], offs)
        other_queries = held.tile([P, n_queries - P], BF16, name="other_queries", align_bytes=ROW_ALIGN)
        nc.sync.dma_start(other_queries[:], queries[:, P:n_queries])

        for b in range(n_blocks):
            block_queries = first_queries[:] if b == 0 else other_queries[:, (b - 1) * P : b * P]
            scores = psum.tile([P, n_landmarks], F32, name="scores")
            nc.tensor.matmul(
                scores[:],
                block_queries,
                keys_sb[:].indirect(offsets[:]),
                start=True,
                stop=True,
            )
            weights = work.tile([P, n_landmarks], F32, name="weights", align_bytes=ROW_ALIGN)
            row_sum = work.tile([P, 1], F32, name="row_sum", align_bytes=ROW_ALIGN)
            nc.scalar.activation(weights[:], scores[:], EXP, accum_out=row_sum[:])
            inv_sum = work.tile([P, 1], F32, name="inv_sum", align_bytes=ROW_ALIGN)
            nc.vector.reciprocal(inv_sum[:], row_sum[:])
            nc.vector.tensor_scalar_mul(weights[:], weights[:], inv_sum[:])
            nc.sync.dma_start(out[b * P : (b + 1) * P, :], weights[:])
